import numpy as np
import ml_dtypes


def mxq(x, axis, fmt="e4m3"):
    dtype, down = {"e4m3": (ml_dtypes.float8_e4m3fn, 7), "e5m2": (ml_dtypes.float8_e5m2, 14)}[fmt]
    v = np.moveaxis(np.asarray(x, np.float32).astype(ml_dtypes.bfloat16).astype(np.float64), axis, -1)
    blocks = v.reshape(v.shape[:-1] + (-1, 32))
    amax = np.abs(blocks).max(-1, keepdims=True)
    byte = np.maximum(np.where(amax > 0, np.frexp(amax)[1] - 1 + 127, 0) - down, 1)
    scale = np.exp2(byte - 127.0)
    codes = (blocks / scale).astype(np.float32).astype(dtype).astype(np.float64)
    return np.moveaxis((codes * scale).reshape(v.shape), -1, axis)


WIDE = False


def mx_kscale(k):
    if not WIDE:
        return np.ones(k)
    levels = np.array([10, -10, 5, -5, 0])
    a = np.random.permutation(np.resize(levels, k // 512 * 4)).reshape(k // 512, 4)
    idx = np.arange(k)
    return np.exp2(a[idx // 512, idx % 128 // 32])


BF16 = ml_dtypes.bfloat16


def bf(x):
    return np.asarray(x, np.float32).astype(BF16)


def f64(x):
    return np.asarray(x).astype(np.float64)


G, B, D, F, O = 2, 128, 8192, 512, 512


def silu(v):
    return v / (1.0 + np.exp(-v))


def setup_inputs():
    s, t = mx_kscale(D), mx_kscale(F)
    return {"x": bf(np.random.standard_normal((B * G, D)) * s),
            "gate_weight": bf(np.random.standard_normal((G, D, F)) / np.sqrt(D) / s[:, None]),
            "up_weight": bf(np.random.standard_normal((G, D, F)) / np.sqrt(D) / s[:, None] * t),
            "down_weight": bf(np.random.standard_normal((G, F, O)) * 1.5 / np.sqrt(F) / t[:, None])}


def reference(x, gate_weight, up_weight, down_weight):
    num_groups = gate_weight.shape[0]
    input_dim = gate_weight.shape[1]
    batch = x.shape[0] // num_groups
    xb = f64(x).reshape(batch, num_groups, input_dim)
    xq = mxq(xb, 2, "e4m3").transpose(1, 0, 2)
    gate = xq @ mxq(f64(gate_weight), 1, "e4m3")
    up = xq @ mxq(f64(up_weight), 1, "e4m3")
    hidden = silu(gate) * up
    out = mxq(hidden, 2, "e4m3") @ mxq(f64(down_weight), 1, "e4m3")
    return out.transpose(1, 0, 2).reshape(-1, down_weight.shape[-1])

@@ -1,0 +1,175 @@
+from contextlib import ExitStack
+
+import concourse.mybir as mybir
+from concourse.masks import make_identity
+
+F32 = mybir.dt.float32
+BF16 = mybir.dt.bfloat16
+U32 = mybir.dt.uint32
+U8 = mybir.dt.uint8
+FP8X4 = mybir.dt.float8_e4m3fn_x4
+
+G, B, D, F, O = 2, 128, 8192, 512, 512
+P = 128
+PACK = 4
+K_PASS = P * PACK
+PASSES = D // K_PASS
+HALVES = 2
+BANK = 512
+
+PIECE_PASSES = 8
+BANK_PASSES = BANK // (HALVES * B)
+RUN = 4
+
+FLOPS = 2 * G * B * (2 * D * F + F * O)
+
+
+def regroup(copy, grouped, rows):
+    copy(
+        out=grouped.rearrange("p (c i) t -> p c t i", i=RUN),
+        in_=rows.rearrange("p t (c i) -> p c t i", i=RUN),
+    )
+
+
+def tile_groupedmlp_plana_k_kernel(tc, x, gate_weight, up_weight, down_weight, out):
+    nc = tc.nc
+    x_by_group = x.rearrange("(b g) d -> b g d", g=G)
+    out_by_group = out.rearrange("(b g) o -> b g o", g=G)
+
+    with ExitStack() as ctx:
+        keep = ctx.enter_context(tc.tile_pool(name="keep", bufs=1))
+        x_stage = ctx.enter_context(tc.tile_pool(name="x_stage", bufs=2))
+        w_rows = ctx.enter_context(tc.tile_pool(name="w_rows", bufs=8))
+        w_stage = ctx.enter_context(tc.tile_pool(name="w_stage", bufs=3))
+        tail = ctx.enter_context(tc.tile_pool(name="tail", bufs=2))
+        sums = ctx.enter_context(tc.psum_pool(name="sums", bufs=2))
+        banks = ctx.enter_context(tc.psum_pool(name="banks", bufs=4))
+
+        ident = keep.tile([P, P], F32)
+        make_identity(nc, ident[:])
+
+        warm_in = keep.tile([P, 1], F32)
+        warm_out = keep.tile([P, 1], F32)
+        nc.vector.memset(warm_in[:], 0.0)
+        nc.scalar.activation(
+            out=warm_out[:], in_=warm_in[:], func=mybir.ActivationFunctionType.Silu
+        )
+
+        x_codes = keep.tile([P, G, PASSES, B], U32, align_bytes=64)
+        x_scales = keep.tile([P, G, PASSES, B], U8, align_bytes=64)
+        for g in range(G):
+            for first in range(0, PASSES, PIECE_PASSES):
+                last = first + PIECE_PASSES
+                x_rows = x_stage.tile([B, PIECE_PASSES * K_PASS], BF16, bufs=4)
+                nc.sync.dma_start(
+                    out=x_rows[:], in_=x_by_group[:, g, first * K_PASS : last * K_PASS]
+                )
+                x_words = x_rows[:].bitcast(F32).rearrange("b (c p u) -> b c u p", p=P, u=HALVES)
+                x_grouped = x_stage.tile([P, PIECE_PASSES * B * PACK], BF16, align_bytes=64)
+                grouped_words = x_grouped[:].bitcast(F32).rearrange(
+                    "p (n c b u) -> p n c b u", c=BANK_PASSES, b=B, u=HALVES
+                )
+                for n in range(PIECE_PASSES // BANK_PASSES):
+                    x_t = banks.tile([P, BANK_PASSES, HALVES, B], F32, tag="bank")
+                    for c in range(BANK_PASSES):
+                        for u in range(HALVES):
+                            nc.tensor.transpose(
+                                x_t[:, c, u, :], x_words[:, n * BANK_PASSES + c, u, :], ident[:]
+                            )
+                    nc.scalar.copy(
+                        out=grouped_words[:, n], in_=x_t[:].rearrange("p c u b -> p c b u")
+                    )
+                nc.vector.quantize_mx(
+                    out=x_codes[:, g, first:last, :].rearrange("p c b -> p (c b)").bitcast(FP8X4),
+                    scales=x_scales[:, g, first:last, :].rearrange("p c b -> p (c b)"),
+                    in_=x_grouped[:],
+                )
+
+        down_grouped = keep.tile([P, G, O, PACK], BF16, align_bytes=64)
+        for g in range(G):
+            down_rows = keep.tile([P, PACK, O], BF16, name="down_rows%d" % g)
+            nc.sync.dma_start(
+                out=down_rows[:], in_=down_weight[g].rearrange("(t p) o -> p t o", p=P)
+            )
+            regroup(nc.vector.tensor_copy, down_grouped[:, g], down_rows[:])
+        down_codes = keep.tile([P, G, O], U32, align_bytes=64)
+        down_scales = keep.tile([P, G, O], U8, align_bytes=64)
+        nc.vector.quantize_mx(
+            out=down_codes[:].rearrange("p g o -> p (g o)").bitcast(FP8X4),
+            scales=down_scales[:].rearrange("p g o -> p (g o)"),
+            in_=down_grouped[:].rearrange("p g o t -> p (g o t)"),
+        )
+
+        def load_pass(weight, g, c, tag):
+            rows = w_rows.tile([P, PACK, F], BF16, tag=tag + "_rows")
+            nc.sync.dma_start(
+                out=rows[:],
+                in_=weight[g, c * K_PASS : (c + 1) * K_PASS, :].rearrange("(p t) f -> p t f", t=PACK),
+            )
+            return rows
+
+        def multiply_pass(grouped, total, g, c, tag):
+            codes = w_stage.tile([P, F], U32, tag=tag + "_codes", align_bytes=64)
+            scales = w_stage.tile([P, F], U8, tag=tag + "_scales", align_bytes=64)
+            nc.vector.quantize_mx(
+                out=codes[:].bitcast(FP8X4),
+                scales=scales[:],
+                in_=grouped[:].rearrange("p f t -> p (f t)"),
+            )
+            nc.tensor.matmul_mx(
+                out=total[:],
+                lhsT=x_codes[:, g, c, :].bitcast(FP8X4),
+                lhsT_scale=x_scales[:, g, c, :],
+                rhs=codes[:].bitcast(FP8X4),
+                rhs_scale=scales[:],
+                start=(c == 0),
+                stop=(c == PASSES - 1),
+            )
+
+        for g in range(G):
+            gate_sum = sums.tile([B, F], F32)
+            up_sum = sums.tile([B, F], F32)
+            for c in range(PASSES):
+                gate_rows = load_pass(gate_weight, g, c, "gate")
+                up_rows = load_pass(up_weight, g, c, "up")
+                gate_grouped = w_stage.tile([P, F, PACK], BF16, align_bytes=64)
+                up_grouped = w_stage.tile([P, F, PACK], BF16, align_bytes=64)
+                regroup(nc.scalar.copy, gate_grouped[:], gate_rows[:])
+                regroup(nc.vector.tensor_copy, up_grouped[:], up_rows[:])
+                multiply_pass(gate_grouped, gate_sum, g, c, "gate")
+                multiply_pass(up_grouped, up_sum, g, c, "up")
+
+            silu = tail.tile([B, F], F32)
+            nc.scalar.activation(
+                out=silu[:], in_=gate_sum[:], func=mybir.ActivationFunctionType.Silu
+            )
+            hidden = tail.tile([B, F], F32)
+            nc.vector.tensor_tensor(
+                out=hidden[:], in0=silu[:], in1=up_sum[:], op=mybir.AluOpType.mult
+            )
+
+            hidden_t = banks.tile([P, PACK, B], F32, tag="bank")
+            for t in range(PACK):
+                nc.tensor.transpose(hidden_t[:, t, :], hidden[:, t * P : (t + 1) * P], ident[:])
+            hidden_grouped = tail.tile([P, B, PACK], BF16, align_bytes=64)
+            nc.scalar.copy(out=hidden_grouped[:], in_=hidden_t[:].rearrange("p t b -> p b t"))
+            hidden_codes = tail.tile([P, B], U32, align_bytes=64)
+            hidden_scales = tail.tile([P, B], U8, align_bytes=64)
+            nc.vector.quantize_mx(
+                out=hidden_codes[:].bitcast(FP8X4),
+                scales=hidden_scales[:],
+                in_=hidden_grouped[:].rearrange("p b t -> p (b t)"),
+            )
+            out_sum = banks.tile([B, O], F32, tag="bank")
+            nc.tensor.matmul_mx(
+                out=out_sum[:],
+                lhsT=hidden_codes[:].bitcast(FP8X4),
+                lhsT_scale=hidden_scales[:],
+                rhs=down_codes[:, g, :].bitcast(FP8X4),
+                rhs_scale=down_scales[:, g, :],
+                start=True,
+                stop=True,
+            )
+            result = tail.tile([B, O], F32)
+            nc.scalar.copy(out=result[:], in_=out_sum[:])
+            nc.sync.dma_start(out=out_by_group[:, g, :], in_=result[:])

@@ -17,8 +17,9 @@ PASSES = D // K_PASS
 HALVES = 2
 BANK = 512
 
-PIECE_PASSES = 8
-BANK_PASSES = BANK // (HALVES * B)
+STEP_PASSES = BANK // (HALVES * B)
+STEPS = PASSES // STEP_PASSES
+PIECE_STEPS = 2
 RUN = 4
 
 FLOPS = 2 * G * B * (2 * D * F + F * O)
@@ -37,9 +38,10 @@ def tile_groupedmlp_plana_k_kernel(tc, x, gate_weight, up_weight, down_weight, o
     out_by_group = out.rearrange("(b g) o -> b g o", g=G)
 
     with ExitStack() as ctx:
+        ctx.enter_context(tc.manual_schedule())
         keep = ctx.enter_context(tc.tile_pool(name="keep", bufs=1))
         x_stage = ctx.enter_context(tc.tile_pool(name="x_stage", bufs=2))
-        w_rows = ctx.enter_context(tc.tile_pool(name="w_rows", bufs=8))
+        w_rows = ctx.enter_context(tc.tile_pool(name="w_rows", bufs=10))
         w_stage = ctx.enter_context(tc.tile_pool(name="w_stage", bufs=3))
         tail = ctx.enter_context(tc.tile_pool(name="tail", bufs=2))
         sums = ctx.enter_context(tc.psum_pool(name="sums", bufs=2))
@@ -57,48 +59,35 @@ def tile_groupedmlp_plana_k_kernel(tc, x, gate_weight, up_weight, down_weight, o
 
         x_codes = keep.tile([P, G, PASSES, B], U32, align_bytes=64)
         x_scales = keep.tile([P, G, PASSES, B], U8, align_bytes=64)
-        for g in range(G):
-            for first in range(0, PASSES, PIECE_PASSES):
-                last = first + PIECE_PASSES
-                x_rows = x_stage.tile([B, PIECE_PASSES * K_PASS], BF16, bufs=4)
-                nc.sync.dma_start(
-                    out=x_rows[:], in_=x_by_group[:, g, first * K_PASS : last * K_PASS]
-                )
-                x_words = x_rows[:].bitcast(F32).rearrange("b (c p u) -> b c u p", p=P, u=HALVES)
-                x_grouped = x_stage.tile([P, PIECE_PASSES * B * PACK], BF16, align_bytes=64)
-                grouped_words = x_grouped[:].bitcast(F32).rearrange(
-                    "p (n c b u) -> p n c b u", c=BANK_PASSES, b=B, u=HALVES
-                )
-                for n in range(PIECE_PASSES // BANK_PASSES):
-                    x_t = banks.tile([P, BANK_PASSES, HALVES, B], F32, tag="bank")
-                    for c in range(BANK_PASSES):
-                        for u in range(HALVES):
-                            nc.tensor.transpose(
-                                x_t[:, c, u, :], x_words[:, n * BANK_PASSES + c, u, :], ident[:]
-                            )
-                    nc.scalar.copy(
-                        out=grouped_words[:, n], in_=x_t[:].rearrange("p c u b -> p c b u")
-                    )
-                nc.vector.quantize_mx(
-                    out=x_codes[:, g, first:last, :].rearrange("p c b -> p (c b)").bitcast(FP8X4),
-                    scales=x_scales[:, g, first:last, :].rearrange("p c b -> p (c b)"),
-                    in_=x_grouped[:],
-                )
 
-        down_grouped = keep.tile([P, G, O, PACK], BF16, align_bytes=64)
-        for g in range(G):
-            down_rows = keep.tile([P, PACK, O], BF16, name="down_rows%d" % g)
-            nc.sync.dma_start(
-                out=down_rows[:], in_=down_weight[g].rearrange("(t p) o -> p t o", p=P)
+        def load_x(g, step):
+            k_first = step * STEP_PASSES * K_PASS
+            k_count = PIECE_STEPS * STEP_PASSES * K_PASS
+            x_rows = x_stage.tile([B, k_count], BF16, bufs=3)
+            nc.sync.dma_start(out=x_rows[:], in_=x_by_group[:, g, k_first : k_first + k_count])
+            return x_rows[:].bitcast(F32).rearrange("b (c p u) -> b c u p", p=P, u=HALVES)
+
+        def transpose_x(x_words, piece_step):
+            x_t = banks.tile([P, STEP_PASSES, HALVES, B], F32, tag="bank")
+            for c in range(STEP_PASSES):
+                for u in range(HALVES):
+                    nc.tensor.transpose(
+                        x_t[:, c, u, :], x_words[:, piece_step * STEP_PASSES + c, u, :], ident[:]
+                    )
+            return x_t
+
+        def quantise_x(x_t, g, step):
+            x_grouped = x_stage.tile([P, STEP_PASSES * B * PACK], BF16, align_bytes=64)
+            nc.scalar.copy(
+                out=x_grouped[:].bitcast(F32).rearrange("p (c b u) -> p c b u", b=B, u=HALVES),
+                in_=x_t[:].rearrange("p c u b -> p c b u"),
             )
-            regroup(nc.vector.tensor_copy, down_grouped[:, g], down_rows[:])
-        down_codes = keep.tile([P, G, O], U32, align_bytes=64)
-        down_scales = keep.tile([P, G, O], U8, align_bytes=64)
-        nc.vector.quantize_mx(
-            out=down_codes[:].rearrange("p g o -> p (g o)").bitcast(FP8X4),
-            scales=down_scales[:].rearrange("p g o -> p (g o)"),
-            in_=down_grouped[:].rearrange("p g o t -> p (g o t)"),
-        )
+            passes = slice(step * STEP_PASSES, (step + 1) * STEP_PASSES)
+            nc.vector.quantize_mx(
+                out=x_codes[:, g, passes, :].rearrange("p c b -> p (c b)").bitcast(FP8X4),
+                scales=x_scales[:, g, passes, :].rearrange("p c b -> p (c b)"),
+                in_=x_grouped[:],
+            )
 
         def load_pass(weight, g, c, tag):
             rows = w_rows.tile([P, PACK, F], BF16, tag=tag + "_rows")
@@ -126,50 +115,98 @@ def tile_groupedmlp_plana_k_kernel(tc, x, gate_weight, up_weight, down_weight, o
                 stop=(c == PASSES - 1),
             )
 
+        def weight_pass(g, c, gate_sum, up_sum):
+            gate_rows = load_pass(gate_weight, g, c, "gate")
+            up_rows = load_pass(up_weight, g, c, "up")
+            gate_grouped = w_stage.tile([P, F, PACK], BF16, align_bytes=64)
+            up_grouped = w_stage.tile([P, F, PACK], BF16, align_bytes=64)
+            regroup(nc.scalar.copy, gate_grouped[:], gate_rows[:])
+            regroup(nc.vector.tensor_copy, up_grouped[:], up_rows[:])
+            multiply_pass(gate_grouped, gate_sum, g, c, "gate")
+            multiply_pass(up_grouped, up_sum, g, c, "up")
+
+        def epilogue(g, gate_sum, up_sum, result):
+            down_rows = tail.tile([P, PACK, O], BF16)
+            down_grouped = tail.tile([P, O, PACK], BF16, align_bytes=64)
+            down_codes = tail.tile([P, O], U32, align_bytes=64)
+            down_scales = tail.tile([P, O], U8, align_bytes=64)
+            silu = tail.tile([B, F], F32)
+            hidden = tail.tile([B, F], F32)
+            hidden_t = banks.tile([P, PACK, B], F32, tag="bank")
+            hidden_grouped = tail.tile([P, B, PACK], BF16, align_bytes=64)
+            hidden_codes = tail.tile([P, B], U32, align_bytes=64)
+            hidden_scales = tail.tile([P, B], U8, align_bytes=64)
+            out_sum = banks.tile([B, O], F32, tag="bank")
+
+            def activate():
+                nc.sync.dma_start(
+                    out=down_rows[:], in_=down_weight[g].rearrange("(t p) o -> p t o", p=P)
+                )
+                nc.scalar.activation(
+                    out=silu[:], in_=gate_sum[:], func=mybir.ActivationFunctionType.Silu
+                )
+                regroup(nc.vector.tensor_copy, down_grouped[:], down_rows[:])
+
+            def multiply_and_transpose():
+                nc.vector.tensor_tensor(
+                    out=hidden[:], in0=silu[:], in1=up_sum[:], op=mybir.AluOpType.mult
+                )
+                for t in range(PACK):
+                    nc.tensor.transpose(hidden_t[:, t, :], hidden[:, t * P : (t + 1) * P], ident[:])
+                nc.vector.quantize_mx(
+                    out=down_codes[:].bitcast(FP8X4),
+                    scales=down_scales[:],
+                    in_=down_grouped[:].rearrange("p o t -> p (o t)"),
+                )
+
+            def round_hidden():
+                nc.scalar.copy(out=hidden_grouped[:], in_=hidden_t[:].rearrange("p t b -> p b t"))
+
+            def second_contraction():
+                nc.vector.quantize_mx(
+                    out=hidden_codes[:].bitcast(FP8X4),
+                    scales=hidden_scales[:],
+                    in_=hidden_grouped[:].rearrange("p b t -> p (b t)"),
+                )
+                nc.tensor.matmul_mx(
+                    out=out_sum[:],
+                    lhsT=hidden_codes[:].bitcast(FP8X4),
+                    lhsT_scale=hidden_scales[:],
+                    rhs=down_codes[:].bitcast(FP8X4),
+                    rhs_scale=down_scales[:],
+                    start=True,
+                    stop=True,
+                )
+
+            def copy_out():
+                nc.scalar.copy(out=result[:], in_=out_sum[:])
+
+            return [activate, multiply_and_transpose, round_hidden, second_contraction, copy_out]
+
+        results = []
+        stages = []
+        x_words = load_x(0, 0)
+        quantise_x(transpose_x(x_words, 0), 0, 0)
         for g in range(G):
             gate_sum = sums.tile([B, F], F32)
             up_sum = sums.tile([B, F], F32)
-            for c in range(PASSES):
-                gate_rows = load_pass(gate_weight, g, c, "gate")
-                up_rows = load_pass(up_weight, g, c, "up")
-                gate_grouped = w_stage.tile([P, F, PACK], BF16, align_bytes=64)
-                up_grouped = w_stage.tile([P, F, PACK], BF16, align_bytes=64)
-                regroup(nc.scalar.copy, gate_grouped[:], gate_rows[:])
-                regroup(nc.vector.tensor_copy, up_grouped[:], up_rows[:])
-                multiply_pass(gate_grouped, gate_sum, g, c, "gate")
-                multiply_pass(up_grouped, up_sum, g, c, "up")
-
-            silu = tail.tile([B, F], F32)
-            nc.scalar.activation(
-                out=silu[:], in_=gate_sum[:], func=mybir.ActivationFunctionType.Silu
-            )
-            hidden = tail.tile([B, F], F32)
-            nc.vector.tensor_tensor(
-                out=hidden[:], in0=silu[:], in1=up_sum[:], op=mybir.AluOpType.mult
-            )
-
-            hidden_t = banks.tile([P, PACK, B], F32, tag="bank")
-            for t in range(PACK):
-                nc.tensor.transpose(hidden_t[:, t, :], hidden[:, t * P : (t + 1) * P], ident[:])
-            hidden_grouped = tail.tile([P, B, PACK], BF16, align_bytes=64)
-            nc.scalar.copy(out=hidden_grouped[:], in_=hidden_t[:].rearrange("p t b -> p b t"))
-            hidden_codes = tail.tile([P, B], U32, align_bytes=64)
-            hidden_scales = tail.tile([P, B], U8, align_bytes=64)
-            nc.vector.quantize_mx(
-                out=hidden_codes[:].bitcast(FP8X4),
-                scales=hidden_scales[:],
-                in_=hidden_grouped[:].rearrange("p b t -> p (b t)"),
-            )
-            out_sum = banks.tile([B, O], F32, tag="bank")
-            nc.tensor.matmul_mx(
-                out=out_sum[:],
-                lhsT=hidden_codes[:].bitcast(FP8X4),
-                lhsT_scale=hidden_scales[:],
-                rhs=down_codes[:, g, :].bitcast(FP8X4),
-                rhs_scale=down_scales[:, g, :],
-                start=True,
-                stop=True,
-            )
+            for step in range(STEPS):
+                next_g, next_step = divmod(g * STEPS + step + 1, STEPS)
+                if next_g < G:
+                    if next_step % PIECE_STEPS == 0:
+                        x_words = load_x(next_g, next_step)
+                    x_t = transpose_x(x_words, next_step % PIECE_STEPS)
+                for c in range(step * STEP_PASSES, (step + 1) * STEP_PASSES):
+                    weight_pass(g, c, gate_sum, up_sum)
+                if next_g < G:
+                    quantise_x(x_t, next_g, next_step)
+                if step < len(stages):
+                    stages[step]()
             result = tail.tile([B, O], F32)
-            nc.scalar.copy(out=result[:], in_=out_sum[:])
-            nc.sync.dma_start(out=out_by_group[:, g, :], in_=result[:])
+            results.append(result)
+            stages = epilogue(g, gate_sum, up_sum, result)
+        for stage in stages:
+            stage()
+
+        for g in range(G):
+            nc.sync.dma_start(out=out_by_group[:, g, :], in_=results[g][:])

@@ -19,8 +19,10 @@ BANK = 512
 
 STEP_PASSES = BANK // (HALVES * B)
 STEPS = PASSES // STEP_PASSES
-PIECE_STEPS = 2
+X_PIECES = (1, 1, 2, 2, 2)
+X_PIECES_NEXT = (2, 2, 2, 2)
 RUN = 4
+HALF = F // 2
 
 FLOPS = 2 * G * B * (2 * D * F + F * O)
 
@@ -41,11 +43,11 @@ def tile_groupedmlp_plana_k_kernel(tc, x, gate_weight, up_weight, down_weight, o
         ctx.enter_context(tc.manual_schedule())
         keep = ctx.enter_context(tc.tile_pool(name="keep", bufs=1))
         x_stage = ctx.enter_context(tc.tile_pool(name="x_stage", bufs=2))
-        w_rows = ctx.enter_context(tc.tile_pool(name="w_rows", bufs=10))
+        w_rows = ctx.enter_context(tc.tile_pool(name="w_rows", bufs=18))
         w_stage = ctx.enter_context(tc.tile_pool(name="w_stage", bufs=3))
         tail = ctx.enter_context(tc.tile_pool(name="tail", bufs=2))
-        sums = ctx.enter_context(tc.psum_pool(name="sums", bufs=2))
-        banks = ctx.enter_context(tc.psum_pool(name="banks", bufs=4))
+        sums = ctx.enter_context(tc.psum_pool(name="sums", bufs=1))
+        banks = ctx.enter_context(tc.psum_pool(name="banks", bufs=5))
 
         ident = keep.tile([P, P], F32)
         make_identity(nc, ident[:])
@@ -60,19 +62,35 @@ def tile_groupedmlp_plana_k_kernel(tc, x, gate_weight, up_weight, down_weight, o
         x_codes = keep.tile([P, G, PASSES, B], U32, align_bytes=64)
         x_scales = keep.tile([P, G, PASSES, B], U8, align_bytes=64)
 
-        def load_x(g, step):
+        def load_x(g, step, steps):
             k_first = step * STEP_PASSES * K_PASS
-            k_count = PIECE_STEPS * STEP_PASSES * K_PASS
-            x_rows = x_stage.tile([B, k_count], BF16, bufs=3)
+            k_count = steps * STEP_PASSES * K_PASS
+            x_rows = x_stage.tile([B, k_count], BF16, bufs=4)
             nc.sync.dma_start(out=x_rows[:], in_=x_by_group[:, g, k_first : k_first + k_count])
             return x_rows[:].bitcast(F32).rearrange("b (c p u) -> b c u p", p=P, u=HALVES)
 
-        def transpose_x(x_words, piece_step):
+        x_words = {}
+        x_starts = {}
+        for g, pieces in enumerate((X_PIECES, X_PIECES_NEXT)):
+            first = 0
+            for count in pieces:
+                x_starts[(g, first)] = count
+                first += count
+
+        def fetch_x(g, step):
+            count = x_starts.get((g, step), 0)
+            if count:
+                words = load_x(g, step, count)
+                for i in range(count):
+                    x_words[(g, step + i)] = (words, i)
+
+        def transpose_x(g, step):
+            words, place = x_words[(g, step)]
             x_t = banks.tile([P, STEP_PASSES, HALVES, B], F32, tag="bank")
             for c in range(STEP_PASSES):
                 for u in range(HALVES):
                     nc.tensor.transpose(
-                        x_t[:, c, u, :], x_words[:, piece_step * STEP_PASSES + c, u, :], ident[:]
+                        x_t[:, c, u, :], words[:, place * STEP_PASSES + c, u, :], ident[:]
                     )
             return x_t
 
@@ -89,78 +107,134 @@ def tile_groupedmlp_plana_k_kernel(tc, x, gate_weight, up_weight, down_weight, o
                 in_=x_grouped[:],
             )
 
-        def load_pass(weight, g, c, tag):
-            rows = w_rows.tile([P, PACK, F], BF16, tag=tag + "_rows")
+        def load_pass(weight, g, c):
+            rows = w_rows.tile([P, PACK, F], BF16)
             nc.sync.dma_start(
                 out=rows[:],
                 in_=weight[g, c * K_PASS : (c + 1) * K_PASS, :].rearrange("(p t) f -> p t f", t=PACK),
             )
             return rows
 
-        def multiply_pass(grouped, total, g, c, tag):
-            codes = w_stage.tile([P, F], U32, tag=tag + "_codes", align_bytes=64)
-            scales = w_stage.tile([P, F], U8, tag=tag + "_scales", align_bytes=64)
+        def quantise_columns(grouped, tag):
+            width = grouped.shape[1]
+            codes = w_stage.tile([P, width], U32, tag=tag + "_codes", align_bytes=64)
+            scales = w_stage.tile([P, width], U8, tag=tag + "_scales", align_bytes=64)
             nc.vector.quantize_mx(
                 out=codes[:].bitcast(FP8X4),
                 scales=scales[:],
                 in_=grouped[:].rearrange("p f t -> p (f t)"),
             )
-            nc.tensor.matmul_mx(
-                out=total[:],
-                lhsT=x_codes[:, g, c, :].bitcast(FP8X4),
-                lhsT_scale=x_scales[:, g, c, :],
-                rhs=codes[:].bitcast(FP8X4),
-                rhs_scale=scales[:],
-                start=(c == 0),
-                stop=(c == PASSES - 1),
-            )
+            return codes, scales
 
-        def weight_pass(g, c, gate_sum, up_sum):
-            gate_rows = load_pass(gate_weight, g, c, "gate")
-            up_rows = load_pass(up_weight, g, c, "up")
-            gate_grouped = w_stage.tile([P, F, PACK], BF16, align_bytes=64)
-            up_grouped = w_stage.tile([P, F, PACK], BF16, align_bytes=64)
-            regroup(nc.scalar.copy, gate_grouped[:], gate_rows[:])
-            regroup(nc.vector.tensor_copy, up_grouped[:], up_rows[:])
-            multiply_pass(gate_grouped, gate_sum, g, c, "gate")
-            multiply_pass(up_grouped, up_sum, g, c, "up")
+        def add_pass(codes, scales, total, g, c):
+            for bank, cols in total:
+                nc.tensor.matmul_mx(
+                    out=bank[:],
+                    lhsT=x_codes[:, g, c, :].bitcast(FP8X4),
+                    lhsT_scale=x_scales[:, g, c, :],
+                    rhs=codes[:, cols].bitcast(FP8X4),
+                    rhs_scale=scales[:, cols],
+                    start=(c == 0),
+                    stop=(c == PASSES - 1),
+                )
 
-        def epilogue(g, gate_sum, up_sum, result):
-            down_rows = tail.tile([P, PACK, O], BF16)
-            down_grouped = tail.tile([P, O, PACK], BF16, align_bytes=64)
-            down_codes = tail.tile([P, O], U32, align_bytes=64)
-            down_scales = tail.tile([P, O], U8, align_bytes=64)
+        def first_step(gate_rows, x_t, gate_sum):
+            for c in range(STEP_PASSES):
+                rows = gate_rows[c]
+                tag = "s" if c % 2 == 0 else "v"
+                grouped = w_stage.tile([P, F, PACK], BF16, tag=tag + "_grouped", align_bytes=64)
+                regroup(nc.vector.tensor_copy, grouped[:, :HALF, :], rows[:, :, :HALF])
+                regroup(nc.scalar.copy, grouped[:, HALF:, :], rows[:, :, HALF:])
+                if c == 0:
+                    quantise_x(x_t, 0, 0)
+                codes, scales = quantise_columns(grouped, tag)
+                add_pass(codes, scales, gate_sum, 0, c)
+
+        def middle_step(rows, total, g, step):
+            c = step * STEP_PASSES
+            s_grouped = w_stage.tile([P, F, PACK], BF16, align_bytes=64)
+            v_grouped = w_stage.tile([P, F, PACK], BF16, align_bytes=64)
+            regroup(nc.scalar.copy, s_grouped[:], rows[0][:])
+            regroup(nc.vector.tensor_copy, v_grouped[:], rows[1][:])
+            codes, scales = quantise_columns(s_grouped, "s")
+            add_pass(codes, scales, total, g, c)
+            codes, scales = quantise_columns(v_grouped, "v")
+            add_pass(codes, scales, total, g, c + 1)
+
+        def last_step(rows, total, g):
+            c = PASSES - STEP_PASSES
+            low_bank, high_bank = total[0][0], total[1][0]
+            whole = slice(0, HALF)
+            lows = [w_stage.tile([P, HALF, PACK], BF16, name=n, tag="v_grouped", align_bytes=64) for n in ("low0", "low1")]
+            highs = [w_stage.tile([P, HALF, PACK], BF16, name=n, tag="s_grouped", align_bytes=64) for n in ("high0", "high1")]
+            for i in range(STEP_PASSES):
+                regroup(nc.scalar.copy, highs[i][:], rows[i][:, :, HALF:])
+            regroup(nc.vector.tensor_copy, lows[0][:], rows[0][:, :, :HALF])
+            low0 = quantise_columns(lows[0], "v")
+            add_pass(*low0, [(low_bank, whole)], g, c)
+            regroup(nc.vector.tensor_copy, lows[1][:], rows[1][:, :, :HALF])
+            high0 = quantise_columns(highs[0], "s")
+            add_pass(*high0, [(high_bank, whole)], g, c)
+            low1 = quantise_columns(lows[1], "v")
+            add_pass(*low1, [(low_bank, whole)], g, c + 1)
+            high1 = quantise_columns(highs[1], "s")
+            add_pass(*high1, [(high_bank, whole)], g, c + 1)
+
+        def prepare_down(g):
+            rows = tail.tile([P, PACK, O], BF16, name="down_rows")
+            grouped = tail.tile([P, O, PACK], BF16, name="down_grouped", align_bytes=64)
+            codes = tail.tile([P, O], U32, name="down_codes", align_bytes=64)
+            scales = tail.tile([P, O], U8, name="down_scales", align_bytes=64)
+            nc.sync.dma_start(out=rows[:], in_=down_weight[g].rearrange("(t p) o -> p t o", p=P))
+
+            def regroup_down():
+                regroup(nc.vector.tensor_copy, grouped[:, :HALF, :], rows[:, :, :HALF])
+                regroup(nc.scalar.copy, grouped[:, HALF:, :], rows[:, :, HALF:])
+
+            def quantise_down():
+                nc.vector.quantize_mx(
+                    out=codes[:].bitcast(FP8X4),
+                    scales=scales[:],
+                    in_=grouped[:].rearrange("p o t -> p (o t)"),
+                )
+
+            return codes, scales, regroup_down, quantise_down
+
+        def activate(gate_sum):
             silu = tail.tile([B, F], F32)
-            hidden = tail.tile([B, F], F32)
-            hidden_t = banks.tile([P, PACK, B], F32, tag="bank")
+            nc.scalar.activation(
+                out=silu[:], in_=gate_sum[0][0][:], func=mybir.ActivationFunctionType.Silu
+            )
+            return silu
+
+        def epilogue(g, silu, up_sum, down):
+            down_codes, down_scales = down[0], down[1]
+            hidden = [tail.tile([B, HALF], F32, name="hidden_low"), tail.tile([B, HALF], F32, name="hidden_high")]
             hidden_grouped = tail.tile([P, B, PACK], BF16, align_bytes=64)
             hidden_codes = tail.tile([P, B], U32, align_bytes=64)
             hidden_scales = tail.tile([P, B], U8, align_bytes=64)
-            out_sum = banks.tile([B, O], F32, tag="bank")
+            result = [tail.tile([B, HALF], F32, name="result_low"), tail.tile([B, HALF], F32, name="result_high")]
+            per_half = PACK // 2
+            hidden_t = []
+            out_sum = []
 
-            def activate():
-                nc.sync.dma_start(
-                    out=down_rows[:], in_=down_weight[g].rearrange("(t p) o -> p t o", p=P)
-                )
-                nc.scalar.activation(
-                    out=silu[:], in_=gate_sum[:], func=mybir.ActivationFunctionType.Silu
-                )
-                regroup(nc.vector.tensor_copy, down_grouped[:], down_rows[:])
-
-            def multiply_and_transpose():
-                nc.vector.tensor_tensor(
-                    out=hidden[:], in0=silu[:], in1=up_sum[:], op=mybir.AluOpType.mult
-                )
-                for t in range(PACK):
-                    nc.tensor.transpose(hidden_t[:, t, :], hidden[:, t * P : (t + 1) * P], ident[:])
-                nc.vector.quantize_mx(
-                    out=down_codes[:].bitcast(FP8X4),
-                    scales=down_scales[:],
-                    in_=down_grouped[:].rearrange("p o t -> p (o t)"),
-                )
+            def multiply():
+                for h in range(2):
+                    cols = slice(h * HALF, (h + 1) * HALF)
+                    nc.vector.tensor_tensor(
+                        out=hidden[h][:], in0=silu[:, cols], in1=up_sum[h][0][:], op=mybir.AluOpType.mult
+                    )
+                    bank = banks.tile([P, per_half, B], F32, name="hidden_t", tag="bank")
+                    hidden_t.append(bank)
+                    for t in range(per_half):
+                        nc.tensor.transpose(bank[:, t, :], hidden[h][:, t * P : (t + 1) * P], ident[:])
 
             def round_hidden():
-                nc.scalar.copy(out=hidden_grouped[:], in_=hidden_t[:].rearrange("p t b -> p b t"))
+                for h in range(2):
+                    nc.scalar.copy(
+                        out=hidden_grouped[:, :, h * per_half : (h + 1) * per_half],
+                        in_=hidden_t[h][:].rearrange("p t b -> p b t"),
+                    )
 
             def second_contraction():
                 nc.vector.quantize_mx(
@@ -168,45 +242,91 @@ def tile_groupedmlp_plana_k_kernel(tc, x, gate_weight, up_weight, down_weight, o
                     scales=hidden_scales[:],
                     in_=hidden_grouped[:].rearrange("p b t -> p (b t)"),
                 )
-                nc.tensor.matmul_mx(
-                    out=out_sum[:],
-                    lhsT=hidden_codes[:].bitcast(FP8X4),
-                    lhsT_scale=hidden_scales[:],
-                    rhs=down_codes[:].bitcast(FP8X4),
-                    rhs_scale=down_scales[:],
-                    start=True,
-                    stop=True,
-                )
+                for h in range(2):
+                    cols = slice(h * HALF, (h + 1) * HALF)
+                    bank = banks.tile([B, HALF], F32, name="out_sum", tag="bank")
+                    out_sum.append(bank)
+                    nc.tensor.matmul_mx(
+                        out=bank[:],
+                        lhsT=hidden_codes[:].bitcast(FP8X4),
+                        lhsT_scale=hidden_scales[:],
+                        rhs=down_codes[:, cols].bitcast(FP8X4),
+                        rhs_scale=down_scales[:, cols],
+                        start=True,
+                        stop=True,
+                    )
 
             def copy_out():
-                nc.scalar.copy(out=result[:], in_=out_sum[:])
+                nc.scalar.copy(out=result[0][:], in_=out_sum[0][:])
+                nc.vector.tensor_copy(out=result[1][:], in_=out_sum[1][:])
 
-            return [activate, multiply_and_transpose, round_hidden, second_contraction, copy_out]
+            def store():
+                for h in range(2):
+                    nc.sync.dma_start(
+                        out=out_by_group[:, g, h * HALF : (h + 1) * HALF], in_=result[h][:]
+                    )
 
-        results = []
+            return [multiply, round_hidden, second_contraction, copy_out], store
+
+        x_ahead = {step - 1: (0, step) for step in range(1, STEPS)}
+        for step in range(STEPS):
+            x_ahead[STEPS + 2 * step] = (1, step)
+
+        sums_of = {}
+        silu_of = {}
+        down_of = {}
+        store_of = {}
         stages = []
-        x_words = load_x(0, 0)
-        quantise_x(transpose_x(x_words, 0), 0, 0)
-        for g in range(G):
-            gate_sum = sums.tile([B, F], F32)
-            up_sum = sums.tile([B, F], F32)
-            for step in range(STEPS):
-                next_g, next_step = divmod(g * STEPS + step + 1, STEPS)
-                if next_g < G:
-                    if next_step % PIECE_STEPS == 0:
-                        x_words = load_x(next_g, next_step)
-                    x_t = transpose_x(x_words, next_step % PIECE_STEPS)
-                for c in range(step * STEP_PASSES, (step + 1) * STEP_PASSES):
-                    weight_pass(g, c, gate_sum, up_sum)
-                if next_g < G:
-                    quantise_x(x_t, next_g, next_step)
-                if step < len(stages):
-                    stages[step]()
-            result = tail.tile([B, O], F32)
-            results.append(result)
-            stages = epilogue(g, gate_sum, up_sum, result)
+        for n in range(2 * G * STEPS):
+            phase, step = divmod(n, STEPS)
+            g, is_up = divmod(phase, 2)
+            weight = up_weight if is_up else gate_weight
+            if step == 0:
+                if is_up:
+                    sums_of[phase] = [
+                        (sums.tile([B, HALF], F32, name="up_low"), slice(0, HALF)),
+                        (sums.tile([B, HALF], F32, name="up_high"), slice(HALF, F)),
+                    ]
+                else:
+                    sums_of[phase] = [(sums.tile([B, F], F32, name="gate_sum"), slice(0, F))]
+            total = sums_of[phase]
+            c = step * STEP_PASSES
+            ahead = x_ahead.get(n)
+            x_t = None
+            if n == 0:
+                rows = [load_pass(weight, g, c)]
+                fetch_x(0, 0)
+                rows.append(load_pass(weight, g, c + 1))
+                fetch_x(0, 1)
+                x_first = transpose_x(0, 0)
+                x_t = transpose_x(0, 1)
+                first_step(rows, x_first, total)
+            else:
+                if ahead:
+                    fetch_x(*ahead)
+                    x_t = transpose_x(*ahead)
+                rows = [load_pass(weight, g, c + i) for i in range(STEP_PASSES)]
+                if n < 2 * G * STEPS - 1:
+                    middle_step(rows, total, g, step)
+                else:
+                    last_step(rows, total, g)
+            if ahead:
+                quantise_x(x_t, *ahead)
+
+            if stages and n % 2 == 1:
+                stages[0]()
+                stages = stages[1:]
+            if is_up and step == 0:
+                silu_of[g] = activate(sums_of[phase - 1])
+            if is_up and step == 1:
+                down_of[g] = prepare_down(g)
+            if is_up and step == 4:
+                down_of[g][2]()
+            if is_up and step == 5:
+                down_of[g][3]()
+            if is_up and step == STEPS - 1:
+                stages, store_of[g] = epilogue(g, silu_of[g], total, down_of[g])
+        store_of[0]()
         for stage in stages:
             stage()
-
-        for g in range(G):
-            nc.sync.dma_start(out=out_by_group[:, g, :], in_=results[g][:])
+        store_of[1]()

@@ -19,10 +19,28 @@ BANK = 512
 
 STEP_PASSES = BANK // (HALVES * B)
 STEPS = PASSES // STEP_PASSES
-X_PIECES = (1, 1, 2, 2, 2)
-X_PIECES_NEXT = (2, 2, 2, 2)
+X_PIECES = ((1, 1, 2, 2, 2), (2, 2, 2, 2))
 RUN = 4
 HALF = F // 2
+TILES = 2 * G * PASSES
+LAG = 1
+LEAD = 2
+TF = 36
+TM = 2
+TR = 0
+SPLIT = 256
+SPLIT_T = 160
+SLEAD = 3
+X_BEFORE = 3
+X_FETCH = 2
+GATE_LEAD = 4
+DOWN_EVERY = 6
+DOWN_LOAD = 10
+DOWN_AT = 22
+X_LAG = 2
+LOAD_AHEAD = 5
+GROUPED_BUFS = 4
+STAGE_EVERY = 3
 
 FLOPS = 2 * G * B * (2 * D * F + F * O)
 
@@ -44,13 +62,16 @@ def tile_groupedmlp_plana_k_kernel(tc, x, gate_weight, up_weight, down_weight, o
         keep = ctx.enter_context(tc.tile_pool(name="keep", bufs=1))
         x_stage = ctx.enter_context(tc.tile_pool(name="x_stage", bufs=2))
         w_rows = ctx.enter_context(tc.tile_pool(name="w_rows", bufs=18))
-        w_stage = ctx.enter_context(tc.tile_pool(name="w_stage", bufs=3))
+        w_stage = ctx.enter_context(tc.tile_pool(name="w_stage", bufs=5))
         tail = ctx.enter_context(tc.tile_pool(name="tail", bufs=2))
         sums = ctx.enter_context(tc.psum_pool(name="sums", bufs=1))
-        banks = ctx.enter_context(tc.psum_pool(name="banks", bufs=5))
+        banks = ctx.enter_context(tc.psum_pool(name="banks", bufs=3))
+        spread = ctx.enter_context(tc.psum_pool(name="spread", bufs=2))
 
         ident = keep.tile([P, P], F32)
         make_identity(nc, ident[:])
+        ident_bf16 = keep.tile([P, P], BF16)
+        nc.vector.tensor_copy(out=ident_bf16[:], in_=ident[:])
 
         warm_in = keep.tile([P, 1], F32)
         warm_out = keep.tile([P, 1], F32)
@@ -70,19 +91,15 @@ def tile_groupedmlp_plana_k_kernel(tc, x, gate_weight, up_weight, down_weight, o
             return x_rows[:].bitcast(F32).rearrange("b (c p u) -> b c u p", p=P, u=HALVES)
 
         x_words = {}
-        x_starts = {}
-        for g, pieces in enumerate((X_PIECES, X_PIECES_NEXT)):
-            first = 0
-            for count in pieces:
-                x_starts[(g, first)] = count
-                first += count
 
         def fetch_x(g, step):
-            count = x_starts.get((g, step), 0)
-            if count:
-                words = load_x(g, step, count)
-                for i in range(count):
-                    x_words[(g, step + i)] = (words, i)
+            first = 0
+            for count in X_PIECES[g]:
+                if first == step:
+                    words = load_x(g, step, count)
+                    for i in range(count):
+                        x_words[(g, step + i)] = (words, i)
+                first += count
 
         def transpose_x(g, step):
             words, place = x_words[(g, step)]
@@ -94,17 +111,20 @@ def tile_groupedmlp_plana_k_kernel(tc, x, gate_weight, up_weight, down_weight, o
                     )
             return x_t
 
-        def quantise_x(x_t, g, step):
-            x_grouped = x_stage.tile([P, STEP_PASSES * B * PACK], BF16, align_bytes=64)
+        def regroup_x(x_t):
+            pairs = x_stage.tile([P, STEP_PASSES * B * PACK], BF16, bufs=3, align_bytes=64)
             nc.scalar.copy(
-                out=x_grouped[:].bitcast(F32).rearrange("p (c b u) -> p c b u", b=B, u=HALVES),
+                out=pairs[:].bitcast(F32).rearrange("p (c b u) -> p c b u", b=B, u=HALVES),
                 in_=x_t[:].rearrange("p c u b -> p c b u"),
             )
+            return pairs
+
+        def quantise_x(pairs, g, step):
             passes = slice(step * STEP_PASSES, (step + 1) * STEP_PASSES)
             nc.vector.quantize_mx(
                 out=x_codes[:, g, passes, :].rearrange("p c b -> p (c b)").bitcast(FP8X4),
                 scales=x_scales[:, g, passes, :].rearrange("p c b -> p (c b)"),
-                in_=x_grouped[:],
+                in_=pairs[:],
             )
 
         def load_pass(weight, g, c):
@@ -138,47 +158,36 @@ def tile_groupedmlp_plana_k_kernel(tc, x, gate_weight, up_weight, down_weight, o
                     stop=(c == PASSES - 1),
                 )
 
-        def first_step(gate_rows, x_t, gate_sum):
-            for c in range(STEP_PASSES):
-                rows = gate_rows[c]
-                tag = "s" if c % 2 == 0 else "v"
-                grouped = w_stage.tile([P, F, PACK], BF16, tag=tag + "_grouped", align_bytes=64)
-                regroup(nc.vector.tensor_copy, grouped[:, :HALF, :], rows[:, :, :HALF])
-                regroup(nc.scalar.copy, grouped[:, HALF:, :], rows[:, :, HALF:])
-                if c == 0:
-                    quantise_x(x_t, 0, 0)
-                codes, scales = quantise_columns(grouped, tag)
-                add_pass(codes, scales, gate_sum, 0, c)
+        def via_tensor(i):
+            return TF <= i < TILES - 2 and i % TM == TR
 
-        def middle_step(rows, total, g, step):
-            c = step * STEP_PASSES
-            s_grouped = w_stage.tile([P, F, PACK], BF16, align_bytes=64)
-            v_grouped = w_stage.tile([P, F, PACK], BF16, align_bytes=64)
-            regroup(nc.scalar.copy, s_grouped[:], rows[0][:])
-            regroup(nc.vector.tensor_copy, v_grouped[:], rows[1][:])
-            codes, scales = quantise_columns(s_grouped, "s")
-            add_pass(codes, scales, total, g, c)
-            codes, scales = quantise_columns(v_grouped, "v")
-            add_pass(codes, scales, total, g, c + 1)
+        def spread_rows(rows):
+            bank = spread.tile([P, HALF, PACK], BF16, name="spread")
+            width = BANK // PACK
+            for first in range(0, HALF, width):
+                nc.tensor.matmul(
+                    out=bank[:, first : first + width, :],
+                    lhsT=ident_bf16[:],
+                    rhs=rows[:, :, HALF + first : HALF + first + width].rearrange("p t f -> p f t"),
+                    start=True,
+                    stop=True,
+                )
+            return bank
 
-        def last_step(rows, total, g):
-            c = PASSES - STEP_PASSES
-            low_bank, high_bank = total[0][0], total[1][0]
-            whole = slice(0, HALF)
-            lows = [w_stage.tile([P, HALF, PACK], BF16, name=n, tag="v_grouped", align_bytes=64) for n in ("low0", "low1")]
-            highs = [w_stage.tile([P, HALF, PACK], BF16, name=n, tag="s_grouped", align_bytes=64) for n in ("high0", "high1")]
-            for i in range(STEP_PASSES):
-                regroup(nc.scalar.copy, highs[i][:], rows[i][:, :, HALF:])
-            regroup(nc.vector.tensor_copy, lows[0][:], rows[0][:, :, :HALF])
-            low0 = quantise_columns(lows[0], "v")
-            add_pass(*low0, [(low_bank, whole)], g, c)
-            regroup(nc.vector.tensor_copy, lows[1][:], rows[1][:, :, :HALF])
-            high0 = quantise_columns(highs[0], "s")
-            add_pass(*high0, [(high_bank, whole)], g, c)
-            low1 = quantise_columns(lows[1], "v")
-            add_pass(*low1, [(low_bank, whole)], g, c + 1)
-            high1 = quantise_columns(highs[1], "s")
-            add_pass(*high1, [(high_bank, whole)], g, c + 1)
+        def last_tile():
+            i = TILES - 1
+            g, is_up, c = order[i]
+            parts = []
+            for n, copy in enumerate((nc.vector.tensor_copy, nc.scalar.copy)):
+                cols = slice(n * HALF, (n + 1) * HALF)
+                tile = w_stage.tile([P, HALF, PACK], BF16, name="grouped_half", bufs=2, align_bytes=64)
+                regroup(copy, tile[:], rows[i][:, :, cols])
+                parts.append(tile)
+            for k in range(i - LAG, i):
+                finish_tile(k)
+            for n in range(2):
+                codes, scales = quantise_columns(parts[n], "w")
+                add_pass(codes, scales, [(sums_of[(g, 1)][n][0], slice(0, HALF))], g, c)
 
         def prepare_down(g):
             rows = tail.tile([P, PACK, O], BF16, name="down_rows")
@@ -268,64 +277,112 @@ def tile_groupedmlp_plana_k_kernel(tc, x, gate_weight, up_weight, down_weight, o
 
             return [multiply, round_hidden, second_contraction, copy_out], store
 
-        x_ahead = {step - 1: (0, step) for step in range(1, STEPS)}
-        for step in range(STEPS):
-            x_ahead[STEPS + 2 * step] = (1, step)
+        order = []
+        for g in range(G):
+            lead = GATE_LEAD if g == G - 1 else 0
+            for c in range(PASSES + lead):
+                if c < PASSES:
+                    order.append((g, 0, c))
+                if c >= lead:
+                    order.append((g, 1, c - lead))
 
+        x_beside = {}
+        for g in range(G):
+            for step in range(STEPS):
+                x_beside[max(0, order.index((g, 0, STEP_PASSES * step)) - X_BEFORE)] = (g, step)
+        assert len(x_beside) == G * STEPS
+        x_after = {n + (X_LAG if n else LAG): n for n in x_beside}
+
+        rows = {}
+        grouped = {}
+        spread_of = {}
+        x_t = {}
+        pairs_of = {}
         sums_of = {}
-        silu_of = {}
-        down_of = {}
-        store_of = {}
-        stages = []
-        for n in range(2 * G * STEPS):
-            phase, step = divmod(n, STEPS)
-            g, is_up = divmod(phase, 2)
-            weight = up_weight if is_up else gate_weight
-            if step == 0:
+
+        def load_tile(i):
+            g, is_up, c = order[i]
+            rows[i] = load_pass(up_weight if is_up else gate_weight, g, c)
+            if i + X_FETCH in x_beside and i:
+                fetch_x(*x_beside[i + X_FETCH])
+            if i == 0:
+                for n in range(X_FETCH + 1):
+                    if n in x_beside:
+                        fetch_x(*x_beside[n])
+
+        def tensor_ahead(i):
+            if i in x_beside:
+                x_t[i] = transpose_x(*x_beside[i])
+
+        def spread_ahead(i):
+            if via_tensor(i):
+                spread_of[i] = spread_rows(rows[i])
+
+        def regroup_tile(i):
+            tile = w_stage.tile([P, F, PACK], BF16, name="grouped", tag="grouped", bufs=GROUPED_BUFS, align_bytes=64)
+            split, end = (SPLIT_T, HALF) if i in spread_of else (SPLIT, F)
+            regroup(nc.vector.tensor_copy, tile[:, :split, :], rows[i][:, :, :split])
+            if split < end:
+                regroup(nc.scalar.copy, tile[:, split:end, :], rows[i][:, :, split:end])
+            if end < F:
+                nc.scalar.copy(out=tile[:, end:, :], in_=spread_of[i][:])
+            grouped[i] = tile
+
+        def finish_tile(i):
+            g, is_up, c = order[i]
+            if c == 0:
                 if is_up:
-                    sums_of[phase] = [
+                    sums_of[(g, 1)] = [
                         (sums.tile([B, HALF], F32, name="up_low"), slice(0, HALF)),
                         (sums.tile([B, HALF], F32, name="up_high"), slice(HALF, F)),
                     ]
                 else:
-                    sums_of[phase] = [(sums.tile([B, F], F32, name="gate_sum"), slice(0, F))]
-            total = sums_of[phase]
-            c = step * STEP_PASSES
-            ahead = x_ahead.get(n)
-            x_t = None
-            if n == 0:
-                rows = [load_pass(weight, g, c)]
-                fetch_x(0, 0)
-                rows.append(load_pass(weight, g, c + 1))
-                fetch_x(0, 1)
-                x_first = transpose_x(0, 0)
-                x_t = transpose_x(0, 1)
-                first_step(rows, x_first, total)
-            else:
-                if ahead:
-                    fetch_x(*ahead)
-                    x_t = transpose_x(*ahead)
-                rows = [load_pass(weight, g, c + i) for i in range(STEP_PASSES)]
-                if n < 2 * G * STEPS - 1:
-                    middle_step(rows, total, g, step)
-                else:
-                    last_step(rows, total, g)
-            if ahead:
-                quantise_x(x_t, *ahead)
+                    sums_of[(g, 0)] = [(sums.tile([B, F], F32, name="gate_sum"), slice(0, F))]
+            codes, scales = quantise_columns(grouped[i], "w")
+            add_pass(codes, scales, sums_of[(g, is_up)], g, c)
 
-            if stages and n % 2 == 1:
-                stages[0]()
-                stages = stages[1:]
-            if is_up and step == 0:
-                silu_of[g] = activate(sums_of[phase - 1])
-            if is_up and step == 1:
-                down_of[g] = prepare_down(g)
-            if is_up and step == 4:
-                down_of[g][2]()
-            if is_up and step == 5:
-                down_of[g][3]()
-            if is_up and step == STEPS - 1:
-                stages, store_of[g] = epilogue(g, silu_of[g], total, down_of[g])
+        silu_of = {}
+        down_of = {}
+        store_of = {}
+        stages = []
+        streamed = TILES - 1
+        for i in range(LOAD_AHEAD):
+            load_tile(i)
+        for i in range(LEAD):
+            tensor_ahead(i)
+        for i in range(streamed):
+            if i + LOAD_AHEAD < TILES:
+                load_tile(i + LOAD_AHEAD)
+            if i + LEAD < streamed:
+                tensor_ahead(i + LEAD)
+            if i + SLEAD < streamed:
+                spread_ahead(i + SLEAD)
+            regroup_tile(i)
+            if i in x_beside:
+                pairs_of[i] = regroup_x(x_t[i])
+            if i in x_after:
+                quantise_x(pairs_of[x_after[i]], *x_beside[x_after[i]])
+            done = i - LAG
+            if done >= 0:
+                finish_tile(done)
+                g, is_up, c = order[done]
+                if stages and done % STAGE_EVERY == STAGE_EVERY - 1:
+                    stages[0]()
+                    stages = stages[1:]
+                for h in range(G):
+                    if done == DOWN_LOAD + DOWN_EVERY * h:
+                        down_of[h] = prepare_down(h)
+                    if done == DOWN_AT + DOWN_EVERY * h:
+                        down_of[h][2]()
+                    if done == DOWN_AT + DOWN_EVERY * h + 2:
+                        down_of[h][3]()
+                if order[done] == (1, 0, 1):
+                    silu_of[0] = activate(sums_of[(0, 0)])
+                    stages, store_of[0] = epilogue(0, silu_of[0], sums_of[(0, 1)], down_of[0])
+                if order[done] == (1, 1, PASSES - 4):
+                    silu_of[1] = activate(sums_of[(1, 0)])
+        last_tile()
+        stages, store_of[1] = epilogue(1, silu_of[1], sums_of[(1, 1)], down_of[1])
         store_of[0]()
         for stage in stages:
             stage()

@@ -34,13 +34,11 @@ SLEAD = 3
 X_BEFORE = 3
 X_FETCH = 2
 GATE_LEAD = 4
-DOWN_EVERY = 6
-DOWN_LOAD = 10
-DOWN_AT = 22
 X_LAG = 2
+D0_SPLIT = 128
+D1_SPLIT = 320
 LOAD_AHEAD = 5
 GROUPED_BUFS = 4
-STAGE_EVERY = 3
 
 FLOPS = 2 * G * B * (2 * D * F + F * O)
 
@@ -189,6 +187,8 @@ def tile_groupedmlp_plana_k_kernel(tc, x, gate_weight, up_weight, down_weight, o
                 codes, scales = quantise_columns(parts[n], "w")
                 add_pass(codes, scales, [(sums_of[(g, 1)][n][0], slice(0, HALF))], g, c)
 
+        down_of = {}
+
         def prepare_down(g):
             rows = tail.tile([P, PACK, O], BF16, name="down_rows")
             grouped = tail.tile([P, O, PACK], BF16, name="down_grouped", align_bytes=64)
@@ -196,9 +196,10 @@ def tile_groupedmlp_plana_k_kernel(tc, x, gate_weight, up_weight, down_weight, o
             scales = tail.tile([P, O], U8, name="down_scales", align_bytes=64)
             nc.sync.dma_start(out=rows[:], in_=down_weight[g].rearrange("(t p) o -> p t o", p=P))
 
-            def regroup_down():
-                regroup(nc.vector.tensor_copy, grouped[:, :HALF, :], rows[:, :, :HALF])
-                regroup(nc.scalar.copy, grouped[:, HALF:, :], rows[:, :, HALF:])
+            def regroup_down(split):
+                if split:
+                    regroup(nc.vector.tensor_copy, grouped[:, :split, :], rows[:, :, :split])
+                regroup(nc.scalar.copy, grouped[:, split:, :], rows[:, :, split:])
 
             def quantise_down():
                 nc.vector.quantize_mx(
@@ -216,8 +217,7 @@ def tile_groupedmlp_plana_k_kernel(tc, x, gate_weight, up_weight, down_weight, o
             )
             return silu
 
-        def epilogue(g, silu, up_sum, down):
-            down_codes, down_scales = down[0], down[1]
+        def epilogue(g, silu, up_sum):
             hidden = [tail.tile([B, HALF], F32, name="hidden_low"), tail.tile([B, HALF], F32, name="hidden_high")]
             hidden_grouped = tail.tile([P, B, PACK], BF16, align_bytes=64)
             hidden_codes = tail.tile([P, B], U32, align_bytes=64)
@@ -245,12 +245,15 @@ def tile_groupedmlp_plana_k_kernel(tc, x, gate_weight, up_weight, down_weight, o
                         in_=hidden_t[h][:].rearrange("p t b -> p b t"),
                     )
 
-            def second_contraction():
+            def quantise_hidden():
                 nc.vector.quantize_mx(
                     out=hidden_codes[:].bitcast(FP8X4),
                     scales=hidden_scales[:],
                     in_=hidden_grouped[:].rearrange("p b t -> p (b t)"),
                 )
+
+            def second_contraction():
+                down_codes, down_scales = down_of[g][:2]
                 for h in range(2):
                     cols = slice(h * HALF, (h + 1) * HALF)
                     bank = banks.tile([B, HALF], F32, name="out_sum", tag="bank")
@@ -275,7 +278,7 @@ def tile_groupedmlp_plana_k_kernel(tc, x, gate_weight, up_weight, down_weight, o
                         out=out_by_group[:, g, h * HALF : (h + 1) * HALF], in_=result[h][:]
                     )
 
-            return [multiply, round_hidden, second_contraction, copy_out], store
+            return multiply, round_hidden, quantise_hidden, second_contraction, copy_out, store
 
         order = []
         for g in range(G):
@@ -342,9 +345,6 @@ def tile_groupedmlp_plana_k_kernel(tc, x, gate_weight, up_weight, down_weight, o
             add_pass(codes, scales, sums_of[(g, is_up)], g, c)
 
         silu_of = {}
-        down_of = {}
-        store_of = {}
-        stages = []
         streamed = TILES - 1
         for i in range(LOAD_AHEAD):
             load_tile(i)
@@ -353,6 +353,8 @@ def tile_groupedmlp_plana_k_kernel(tc, x, gate_weight, up_weight, down_weight, o
         for i in range(streamed):
             if i + LOAD_AHEAD < TILES:
                 load_tile(i + LOAD_AHEAD)
+            elif i + LOAD_AHEAD < TILES + G:
+                down_of[i + LOAD_AHEAD - TILES] = prepare_down(i + LOAD_AHEAD - TILES)
             if i + LEAD < streamed:
                 tensor_ahead(i + LEAD)
             if i + SLEAD < streamed:
@@ -365,25 +367,28 @@ def tile_groupedmlp_plana_k_kernel(tc, x, gate_weight, up_weight, down_weight, o
             done = i - LAG
             if done >= 0:
                 finish_tile(done)
-                g, is_up, c = order[done]
-                if stages and done % STAGE_EVERY == STAGE_EVERY - 1:
-                    stages[0]()
-                    stages = stages[1:]
-                for h in range(G):
-                    if done == DOWN_LOAD + DOWN_EVERY * h:
-                        down_of[h] = prepare_down(h)
-                    if done == DOWN_AT + DOWN_EVERY * h:
-                        down_of[h][2]()
-                    if done == DOWN_AT + DOWN_EVERY * h + 2:
-                        down_of[h][3]()
                 if order[done] == (1, 0, 1):
                     silu_of[0] = activate(sums_of[(0, 0)])
-                    stages, store_of[0] = epilogue(0, silu_of[0], sums_of[(0, 1)], down_of[0])
+                    first = epilogue(0, silu_of[0], sums_of[(0, 1)])
+                    first[0]()
+                if order[done] == (1, 0, 3):
+                    first[1]()
+                if order[done] == (1, 0, 5):
+                    first[2]()
                 if order[done] == (1, 1, PASSES - 4):
                     silu_of[1] = activate(sums_of[(1, 0)])
         last_tile()
-        stages, store_of[1] = epilogue(1, silu_of[1], sums_of[(1, 1)], down_of[1])
-        store_of[0]()
-        for stage in stages:
-            stage()
-        store_of[1]()
+        second = epilogue(1, silu_of[1], sums_of[(1, 1)])
+        down_of[0][2](D0_SPLIT)
+        second[0]()
+        down_of[1][2](D1_SPLIT)
+        second[1]()
+        down_of[0][3]()
+        first[3]()
+        down_of[1][3]()
+        second[2]()
+        first[4]()
+        first[5]()
+        second[3]()
+        second[4]()
+        second[5]()

@@ -29,14 +29,14 @@ TF = 36
 TM = 2
 TR = 0
 SPLIT = 256
-SPLIT_T = 160
+SPLIT_T = 208
 SLEAD = 3
 X_BEFORE = 3
 X_FETCH = 2
 GATE_LEAD = 4
 X_LAG = 2
 D0_SPLIT = 128
-D1_SPLIT = 320
+D1_SPLIT = 256
 LOAD_AHEAD = 5
 GROUPED_BUFS = 4
 

from contextlib import ExitStack

import concourse.mybir as mybir
from concourse.masks import make_identity

F32 = mybir.dt.float32
BF16 = mybir.dt.bfloat16
U32 = mybir.dt.uint32
U8 = mybir.dt.uint8
FP8X4 = mybir.dt.float8_e4m3fn_x4

G, B, D, F, O = 2, 128, 8192, 512, 512
P = 128
PACK = 4
K_PASS = P * PACK
PASSES = D // K_PASS
HALVES = 2
BANK = 512

STEP_PASSES = BANK // (HALVES * B)
STEPS = PASSES // STEP_PASSES
X_PIECES = ((1, 1, 2, 2, 2), (2, 2, 2, 2))
RUN = 4
HALF = F // 2
TILES = 2 * G * PASSES
LAG = 1
LEAD = 2
TF = 36
TM = 2
TR = 0
SPLIT = 256
SPLIT_T = 208
SLEAD = 3
X_BEFORE = 3
X_FETCH = 2
GATE_LEAD = 4
X_LAG = 2
D0_SPLIT = 128
D1_SPLIT = 256
LOAD_AHEAD = 5
GROUPED_BUFS = 4

FLOPS = 2 * G * B * (2 * D * F + F * O)


def regroup(copy, grouped, rows):
    copy(
        out=grouped.rearrange("p (c i) t -> p c t i", i=RUN),
        in_=rows.rearrange("p t (c i) -> p c t i", i=RUN),
    )


def tile_groupedmlp_plana_k_kernel(tc, x, gate_weight, up_weight, down_weight, out):
    nc = tc.nc
    x_by_group = x.rearrange("(b g) d -> b g d", g=G)
    out_by_group = out.rearrange("(b g) o -> b g o", g=G)

    with ExitStack() as ctx:
        ctx.enter_context(tc.manual_schedule())
        keep = ctx.enter_context(tc.tile_pool(name="keep", bufs=1))
        x_stage = ctx.enter_context(tc.tile_pool(name="x_stage", bufs=2))
        w_rows = ctx.enter_context(tc.tile_pool(name="w_rows", bufs=18))
        w_stage = ctx.enter_context(tc.tile_pool(name="w_stage", bufs=5))
        tail = ctx.enter_context(tc.tile_pool(name="tail", bufs=2))
        sums = ctx.enter_context(tc.psum_pool(name="sums", bufs=1))
        banks = ctx.enter_context(tc.psum_pool(name="banks", bufs=3))
        spread = ctx.enter_context(tc.psum_pool(name="spread", bufs=2))

        ident = keep.tile([P, P], F32)
        make_identity(nc, ident[:])
        ident_bf16 = keep.tile([P, P], BF16)
        nc.vector.tensor_copy(out=ident_bf16[:], in_=ident[:])

        warm_in = keep.tile([P, 1], F32)
        warm_out = keep.tile([P, 1], F32)
        nc.vector.memset(warm_in[:], 0.0)
        nc.scalar.activation(
            out=warm_out[:], in_=warm_in[:], func=mybir.ActivationFunctionType.Silu
        )

        x_codes = keep.tile([P, G, PASSES, B], U32, align_bytes=64)
        x_scales = keep.tile([P, G, PASSES, B], U8, align_bytes=64)

        def load_x(g, step, steps):
            k_first = step * STEP_PASSES * K_PASS
            k_count = steps * STEP_PASSES * K_PASS
            x_rows = x_stage.tile([B, k_count], BF16, bufs=4)
            nc.sync.dma_start(out=x_rows[:], in_=x_by_group[:, g, k_first : k_first + k_count])
            return x_rows[:].bitcast(F32).rearrange("b (c p u) -> b c u p", p=P, u=HALVES)

        x_words = {}

        def fetch_x(g, step):
            first = 0
            for count in X_PIECES[g]:
                if first == step:
                    words = load_x(g, step, count)
                    for i in range(count):
                        x_words[(g, step + i)] = (words, i)
                first += count

        def transpose_x(g, step):
            words, place = x_words[(g, step)]
            x_t = banks.tile([P, STEP_PASSES, HALVES, B], F32, tag="bank")
            for c in range(STEP_PASSES):
                for u in range(HALVES):
                    nc.tensor.transpose(
                        x_t[:, c, u, :], words[:, place * STEP_PASSES + c, u, :], ident[:]
                    )
            return x_t

        def regroup_x(x_t):
            pairs = x_stage.tile([P, STEP_PASSES * B * PACK], BF16, bufs=3, align_bytes=64)
            nc.scalar.copy(
                out=pairs[:].bitcast(F32).rearrange("p (c b u) -> p c b u", b=B, u=HALVES),
                in_=x_t[:].rearrange("p c u b -> p c b u"),
            )
            return pairs

        def quantise_x(pairs, g, step):
            passes = slice(step * STEP_PASSES, (step + 1) * STEP_PASSES)
            nc.vector.quantize_mx(
                out=x_codes[:, g, passes, :].rearrange("p c b -> p (c b)").bitcast(FP8X4),
                scales=x_scales[:, g, passes, :].rearrange("p c b -> p (c b)"),
                in_=pairs[:],
            )

        def load_pass(weight, g, c):
            rows = w_rows.tile([P, PACK, F], BF16)
            nc.sync.dma_start(
                out=rows[:],
                in_=weight[g, c * K_PASS : (c + 1) * K_PASS, :].rearrange("(p t) f -> p t f", t=PACK),
            )
            return rows

        def quantise_columns(grouped, tag):
            width = grouped.shape[1]
            codes = w_stage.tile([P, width], U32, tag=tag + "_codes", align_bytes=64)
            scales = w_stage.tile([P, width], U8, tag=tag + "_scales", align_bytes=64)
            nc.vector.quantize_mx(
                out=codes[:].bitcast(FP8X4),
                scales=scales[:],
                in_=grouped[:].rearrange("p f t -> p (f t)"),
            )
            return codes, scales

        def add_pass(codes, scales, total, g, c):
            for bank, cols in total:
                nc.tensor.matmul_mx(
                    out=bank[:],
                    lhsT=x_codes[:, g, c, :].bitcast(FP8X4),
                    lhsT_scale=x_scales[:, g, c, :],
                    rhs=codes[:, cols].bitcast(FP8X4),
                    rhs_scale=scales[:, cols],
                    start=(c == 0),
                    stop=(c == PASSES - 1),
                )

        def via_tensor(i):
            return TF <= i < TILES - 2 and i % TM == TR

        def spread_rows(rows):
            bank = spread.tile([P, HALF, PACK], BF16, name="spread")
            width = BANK // PACK
            for first in range(0, HALF, width):
                nc.tensor.matmul(
                    out=bank[:, first : first + width, :],
                    lhsT=ident_bf16[:],
                    rhs=rows[:, :, HALF + first : HALF + first + width].rearrange("p t f -> p f t"),
                    start=True,
                    stop=True,
                )
            return bank

        def last_tile():
            i = TILES - 1
            g, is_up, c = order[i]
            parts = []
            for n, copy in enumerate((nc.vector.tensor_copy, nc.scalar.copy)):
                cols = slice(n * HALF, (n + 1) * HALF)
                tile = w_stage.tile([P, HALF, PACK], BF16, name="grouped_half", bufs=2, align_bytes=64)
                regroup(copy, tile[:], rows[i][:, :, cols])
                parts.append(tile)
            for k in range(i - LAG, i):
                finish_tile(k)
            for n in range(2):
                codes, scales = quantise_columns(parts[n], "w")
                add_pass(codes, scales, [(sums_of[(g, 1)][n][0], slice(0, HALF))], g, c)

        down_of = {}

        def prepare_down(g):
            rows = tail.tile([P, PACK, O], BF16, name="down_rows")
            grouped = tail.tile([P, O, PACK], BF16, name="down_grouped", align_bytes=64)
            codes = tail.tile([P, O], U32, name="down_codes", align_bytes=64)
            scales = tail.tile([P, O], U8, name="down_scales", align_bytes=64)
            nc.sync.dma_start(out=rows[:], in_=down_weight[g].rearrange("(t p) o -> p t o", p=P))

            def regroup_down(split):
                if split:
                    regroup(nc.vector.tensor_copy, grouped[:, :split, :], rows[:, :, :split])
                regroup(nc.scalar.copy, grouped[:, split:, :], rows[:, :, split:])

            def quantise_down():
                nc.vector.quantize_mx(
                    out=codes[:].bitcast(FP8X4),
                    scales=scales[:],
                    in_=grouped[:].rearrange("p o t -> p (o t)"),
                )

            return codes, scales, regroup_down, quantise_down

        def activate(gate_sum):
            silu = tail.tile([B, F], F32)
            nc.scalar.activation(
                out=silu[:], in_=gate_sum[0][0][:], func=mybir.ActivationFunctionType.Silu
            )
            return silu

        def epilogue(g, silu, up_sum):
            hidden = [tail.tile([B, HALF], F32, name="hidden_low"), tail.tile([B, HALF], F32, name="hidden_high")]
            hidden_grouped = tail.tile([P, B, PACK], BF16, align_bytes=64)
            hidden_codes = tail.tile([P, B], U32, align_bytes=64)
            hidden_scales = tail.tile([P, B], U8, align_bytes=64)
            result = [tail.tile([B, HALF], F32, name="result_low"), tail.tile([B, HALF], F32, name="result_high")]
            per_half = PACK // 2
            hidden_t = []
            out_sum = []

            def multiply():
                for h in range(2):
                    cols = slice(h * HALF, (h + 1) * HALF)
                    nc.vector.tensor_tensor(
                        out=hidden[h][:], in0=silu[:, cols], in1=up_sum[h][0][:], op=mybir.AluOpType.mult
                    )
                    bank = banks.tile([P, per_half, B], F32, name="hidden_t", tag="bank")
                    hidden_t.append(bank)
                    for t in range(per_half):
                        nc.tensor.transpose(bank[:, t, :], hidden[h][:, t * P : (t + 1) * P], ident[:])

            def round_hidden():
                for h in range(2):
                    nc.scalar.copy(
                        out=hidden_grouped[:, :, h * per_half : (h + 1) * per_half],
                        in_=hidden_t[h][:].rearrange("p t b -> p b t"),
                    )

            def quantise_hidden():
                nc.vector.quantize_mx(
                    out=hidden_codes[:].bitcast(FP8X4),
                    scales=hidden_scales[:],
                    in_=hidden_grouped[:].rearrange("p b t -> p (b t)"),
                )

            def second_contraction():
                down_codes, down_scales = down_of[g][:2]
                for h in range(2):
                    cols = slice(h * HALF, (h + 1) * HALF)
                    bank = banks.tile([B, HALF], F32, name="out_sum", tag="bank")
                    out_sum.append(bank)
                    nc.tensor.matmul_mx(
                        out=bank[:],
                        lhsT=hidden_codes[:].bitcast(FP8X4),
                        lhsT_scale=hidden_scales[:],
                        rhs=down_codes[:, cols].bitcast(FP8X4),
                        rhs_scale=down_scales[:, cols],
                        start=True,
                        stop=True,
                    )

            def copy_out():
                nc.scalar.copy(out=result[0][:], in_=out_sum[0][:])
                nc.vector.tensor_copy(out=result[1][:], in_=out_sum[1][:])

            def store():
                for h in range(2):
                    nc.sync.dma_start(
                        out=out_by_group[:, g, h * HALF : (h + 1) * HALF], in_=result[h][:]
                    )

            return multiply, round_hidden, quantise_hidden, second_contraction, copy_out, store

        order = []
        for g in range(G):
            lead = GATE_LEAD if g == G - 1 else 0
            for c in range(PASSES + lead):
                if c < PASSES:
                    order.append((g, 0, c))
                if c >= lead:
                    order.append((g, 1, c - lead))

        x_beside = {}
        for g in range(G):
            for step in range(STEPS):
                x_beside[max(0, order.index((g, 0, STEP_PASSES * step)) - X_BEFORE)] = (g, step)
        assert len(x_beside) == G * STEPS
        x_after = {n + (X_LAG if n else LAG): n for n in x_beside}

        rows = {}
        grouped = {}
        spread_of = {}
        x_t = {}
        pairs_of = {}
        sums_of = {}

        def load_tile(i):
            g, is_up, c = order[i]
            rows[i] = load_pass(up_weight if is_up else gate_weight, g, c)
            if i + X_FETCH in x_beside and i:
                fetch_x(*x_beside[i + X_FETCH])
            if i == 0:
                for n in range(X_FETCH + 1):
                    if n in x_beside:
                        fetch_x(*x_beside[n])

        def tensor_ahead(i):
            if i in x_beside:
                x_t[i] = transpose_x(*x_beside[i])

        def spread_ahead(i):
            if via_tensor(i):
                spread_of[i] = spread_rows(rows[i])

        def regroup_tile(i):
            tile = w_stage.tile([P, F, PACK], BF16, name="grouped", tag="grouped", bufs=GROUPED_BUFS, align_bytes=64)
            split, end = (SPLIT_T, HALF) if i in spread_of else (SPLIT, F)
            regroup(nc.vector.tensor_copy, tile[:, :split, :], rows[i][:, :, :split])
            if split < end:
                regroup(nc.scalar.copy, tile[:, split:end, :], rows[i][:, :, split:end])
            if end < F:
                nc.scalar.copy(out=tile[:, end:, :], in_=spread_of[i][:])
            grouped[i] = tile

        def finish_tile(i):
            g, is_up, c = order[i]
            if c == 0:
                if is_up:
                    sums_of[(g, 1)] = [
                        (sums.tile([B, HALF], F32, name="up_low"), slice(0, HALF)),
                        (sums.tile([B, HALF], F32, name="up_high"), slice(HALF, F)),
                    ]
                else:
                    sums_of[(g, 0)] = [(sums.tile([B, F], F32, name="gate_sum"), slice(0, F))]
            codes, scales = quantise_columns(grouped[i], "w")
            add_pass(codes, scales, sums_of[(g, is_up)], g, c)

        silu_of = {}
        streamed = TILES - 1
        for i in range(LOAD_AHEAD):
            load_tile(i)
        for i in range(LEAD):
            tensor_ahead(i)
        for i in range(streamed):
            if i + LOAD_AHEAD < TILES:
                load_tile(i + LOAD_AHEAD)
            elif i + LOAD_AHEAD < TILES + G:
                down_of[i + LOAD_AHEAD - TILES] = prepare_down(i + LOAD_AHEAD - TILES)
            if i + LEAD < streamed:
                tensor_ahead(i + LEAD)
            if i + SLEAD < streamed:
                spread_ahead(i + SLEAD)
            regroup_tile(i)
            if i in x_beside:
                pairs_of[i] = regroup_x(x_t[i])
            if i in x_after:
                quantise_x(pairs_of[x_after[i]], *x_beside[x_after[i]])
            done = i - LAG
            if done >= 0:
                finish_tile(done)
                if order[done] == (1, 0, 1):
                    silu_of[0] = activate(sums_of[(0, 0)])
                    first = epilogue(0, silu_of[0], sums_of[(0, 1)])
                    first[0]()
                if order[done] == (1, 0, 3):
                    first[1]()
                if order[done] == (1, 0, 5):
                    first[2]()
                if order[done] == (1, 1, PASSES - 4):
                    silu_of[1] = activate(sums_of[(1, 0)])
        last_tile()
        second = epilogue(1, silu_of[1], sums_of[(1, 1)])
        down_of[0][2](D0_SPLIT)
        second[0]()
        down_of[1][2](D1_SPLIT)
        second[1]()
        down_of[0][3]()
        first[3]()
        down_of[1][3]()
        second[2]()
        first[4]()
        first[5]()
        second[3]()
        second[4]()
        second[5]()
